import numpy as np
import ml_dtypes


def mxq(x, axis, fmt="e4m3"):
    dtype, down = {"e4m3": (ml_dtypes.float8_e4m3fn, 7), "e5m2": (ml_dtypes.float8_e5m2, 14)}[fmt]
    v = np.moveaxis(np.asarray(x, np.float32).astype(ml_dtypes.bfloat16).astype(np.float64), axis, -1)
    blocks = v.reshape(v.shape[:-1] + (-1, 32))
    amax = np.abs(blocks).max(-1, keepdims=True)
    byte = np.maximum(np.where(amax > 0, np.frexp(amax)[1] - 1 + 127, 0) - down, 1)
    scale = np.exp2(byte - 127.0)
    codes = (blocks / scale).astype(np.float32).astype(dtype).astype(np.float64)
    return np.moveaxis((codes * scale).reshape(v.shape), -1, axis)


WIDE = False


def mx_kscale(k):
    if not WIDE:
        return np.ones(k)
    levels = np.array([20, -20, 10, -10, 0])
    a = np.random.permutation(np.resize(levels, k // 512 * 4)).reshape(k // 512, 4)
    idx = np.arange(k)
    return np.exp2(a[idx // 512, idx % 128 // 32])


BF16 = ml_dtypes.bfloat16


def bf(x):
    return np.asarray(x, np.float32).astype(BF16)


def f64(x):
    return np.asarray(x).astype(np.float64)


M, I, O = 4096, 1024, 512
SPARSITY = 0.98
GSCALE = 4.0


def _build_mask():
    num_connections = int((1 - SPARSITY) * I * O)
    cpn = max(1, num_connections // O)
    rows = np.arange(O)[:, None]
    cols = (rows * cpn + np.arange(cpn)[None, :]) % I
    mask = np.zeros((O, I))
    mask[np.repeat(np.arange(O), cpn), cols.reshape(-1)] = 1.0
    return mask, cpn


def setup_inputs():
    u = mx_kscale(O)
    mask_np, cpn = _build_mask()
    x = np.random.standard_normal((M, I))
    weight = np.random.standard_normal((O, I)) * np.sqrt(2.0 / cpn) / u[:, None]
    bias = np.random.standard_normal(O) * 0.1
    g = np.random.standard_normal((M, O)) * np.exp2(np.random.randint(-12, 1, (M, 1))) * GSCALE * u[None, :]
    return {"x": bf(x), "weight": bf(weight), "bias": bf(bias), "mask": bf(mask_np), "grad_out": bf(g)}


def reference(x, weight, bias, mask, grad_out):
    masked_weight = f64(weight) * f64(mask)
    return mxq(f64(grad_out), 1, "e5m2") @ mxq(masked_weight, 0, "e4m3")

@@ -1,0 +1,134 @@
+from contextlib import ExitStack
+
+import concourse.mybir as mybir
+from concourse.masks import make_identity
+
+BF16 = mybir.dt.bfloat16
+F32 = mybir.dt.float32
+U32 = mybir.dt.uint32
+U8 = mybir.dt.uint8
+E4M3_X4 = mybir.dt.float8_e4m3fn_x4
+E5M2_X4 = mybir.dt.float8_e5m2_x4
+
+TOKENS, IN_FEATURES, OUT_FEATURES = 4096, 1024, 512
+FLOPS = 2 * TOKENS * IN_FEATURES * OUT_FEATURES
+BYTES = 2 * (TOKENS * OUT_FEATURES + 2 * OUT_FEATURES * IN_FEATURES) + 4 * TOKENS * IN_FEATURES
+
+P = 128
+PACK = 4
+assert OUT_FEATURES == P * PACK
+K_HALF = OUT_FEATURES // 2
+N_PASS = 512
+COLUMN_HALVES = IN_FEATURES // N_PASS
+
+TOKEN_TILES = TOKENS // P
+GROUP = 2
+N_GROUPS = TOKEN_TILES // GROUP
+LOAD_TILES = 8
+N_LOADS = TOKEN_TILES // LOAD_TILES
+
+
+def tile_structuredconnection_t_kernel(tc, x, weight, bias, mask, grad_out, out):
+    nc = tc.nc
+    grad_by_tile = grad_out.rearrange("(p t) k -> p t k", t=TOKEN_TILES)
+    out_by_tile = out.rearrange("(p t) i -> p t i", t=TOKEN_TILES)
+
+    with ExitStack() as stack:
+        keep = stack.enter_context(tc.tile_pool(name="keep", bufs=1))
+        stage = stack.enter_context(tc.tile_pool(name="stage", bufs=3))
+        results = stack.enter_context(tc.tile_pool(name="results", bufs=4))
+        flipped_banks = stack.enter_context(tc.psum_pool(name="flipped_banks", bufs=2))
+        product_banks = stack.enter_context(tc.psum_pool(name="product_banks", bufs=6))
+        stack.enter_context(tc.manual_schedule())
+
+        weight_raw, mask_raw = [], []
+        for u in range(2):
+            rows = slice(u * K_HALF, (u + 1) * K_HALF)
+            w_raw = keep.tile([P, 2, IN_FEATURES], BF16, name="w_raw%d" % u)
+            m_raw = keep.tile([P, 2, IN_FEATURES], BF16, name="m_raw%d" % u)
+            nc.sync.dma_start(out=w_raw[:], in_=weight[rows, :].rearrange("(p e) c -> p e c", e=2))
+            nc.sync.dma_start(out=m_raw[:], in_=mask[rows, :].rearrange("(p e) c -> p e c", e=2))
+            weight_raw.append(w_raw)
+            mask_raw.append(m_raw)
+        grad_raw = []
+        for c in range(N_LOADS):
+            g_raw = keep.tile([P, LOAD_TILES, OUT_FEATURES], BF16, name="g_raw%d" % c)
+            nc.sync.dma_start(out=g_raw[:], in_=grad_by_tile[:, c * LOAD_TILES : (c + 1) * LOAD_TILES, :])
+            grad_raw.append(g_raw)
+
+        identity = keep.tile([P, P], F32, name="identity")
+        make_identity(nc, identity[:])
+
+        masked = keep.tile([P, PACK, IN_FEATURES], BF16, name="masked")
+        for u in range(2):
+            nc.vector.tensor_tensor(
+                out=masked[:, 2 * u : 2 * u + 2, :],
+                in0=weight_raw[u][:],
+                in1=mask_raw[u][:],
+                op=mybir.AluOpType.mult,
+            )
+        w_grouped = keep.tile([P, IN_FEATURES, PACK], BF16, name="w_grouped", align_bytes=64)
+        w_codes = keep.tile([P, IN_FEATURES], U32, name="w_codes", align_bytes=64)
+        w_scales = keep.tile([P, IN_FEATURES], U8, name="w_scales", align_bytes=64)
+        column_halves = [slice(h * N_PASS, (h + 1) * N_PASS) for h in range(COLUMN_HALVES)]
+        for cols in column_halves:
+            nc.vector.tensor_copy(
+                out=w_grouped[:, cols, :], in_=masked[:, :, cols].rearrange("p t c -> p c t")
+            )
+        for cols in column_halves:
+            nc.vector.quantize_mx(
+                out=w_codes[:, cols].bitcast(E4M3_X4),
+                scales=w_scales[:, cols],
+                in_=w_grouped[:, cols, :].rearrange("p c t -> p (c t)"),
+            )
+
+        def transpose_group(g):
+            flipped = flipped_banks.tile([P, GROUP, 2, P], F32, name="flipped")
+            for a in range(GROUP):
+                t = g * GROUP + a
+                words = grad_raw[t // LOAD_TILES][:].bitcast(F32)[:, t % LOAD_TILES, :]
+                for u in range(2):
+                    nc.tensor.transpose(flipped[:, a, u, :], words[:, u * P : (u + 1) * P], identity[:])
+            g_grouped = stage.tile([P, GROUP, P, PACK], BF16, name="g_grouped", align_bytes=64)
+            nc.scalar.copy(out=g_grouped[:].bitcast(F32), in_=flipped[:].rearrange("p a u r -> p a r u"))
+            return g_grouped
+
+        def quantise_group(g_grouped):
+            g_codes = stage.tile([P, GROUP * P], U32, name="g_codes", align_bytes=64)
+            g_scales = stage.tile([P, GROUP * P], U8, name="g_scales", align_bytes=64)
+            nc.vector.quantize_mx(
+                out=g_codes[:].bitcast(E5M2_X4),
+                scales=g_scales[:],
+                in_=g_grouped[:].rearrange("p a r t -> p (a r t)"),
+            )
+            return g_codes, g_scales
+
+        def multiply_group(g, g_codes, g_scales):
+            result = results.tile([P, GROUP, IN_FEATURES], F32, name="result")
+            for a in range(GROUP):
+                tokens = slice(a * P, (a + 1) * P)
+                for h, cols in enumerate(column_halves):
+                    product = product_banks.tile([P, N_PASS], F32, name="product")
+                    nc.tensor.matmul_mx(
+                        out=product[:],
+                        lhsT=g_codes[:, tokens].bitcast(E5M2_X4),
+                        lhsT_scale=g_scales[:, tokens],
+                        rhs=w_codes[:, cols].bitcast(E4M3_X4),
+                        rhs_scale=w_scales[:, cols],
+                        start=True,
+                        stop=True,
+                    )
+                    if h == 0:
+                        nc.scalar.copy(out=result[:, a, cols], in_=product[:])
+                    else:
+                        nc.vector.tensor_copy(out=result[:, a, cols], in_=product[:])
+            nc.sync.dma_start(out=out_by_tile[:, g * GROUP : (g + 1) * GROUP, :], in_=result[:])
+
+        grouped = {0: transpose_group(0), 1: transpose_group(1)}
+        quantised = {0: quantise_group(grouped[0])}
+        for g in range(N_GROUPS):
+            if g + 2 < N_GROUPS:
+                grouped[g + 2] = transpose_group(g + 2)
+            if g + 1 < N_GROUPS:
+                quantised[g + 1] = quantise_group(grouped[g + 1])
+            multiply_group(g, quantised[g][0], quantised[g][1])

@@ -24,7 +24,7 @@ COLUMN_HALVES = IN_FEATURES // N_PASS
 TOKEN_TILES = TOKENS // P
 GROUP = 2
 N_GROUPS = TOKEN_TILES // GROUP
-LOAD_TILES = 8
+LOAD_TILES = 4
 N_LOADS = TOKEN_TILES // LOAD_TILES
 
 
@@ -41,6 +41,14 @@ def tile_structuredconnection_t_kernel(tc, x, weight, bias, mask, grad_out, out)
         product_banks = stack.enter_context(tc.psum_pool(name="product_banks", bufs=6))
         stack.enter_context(tc.manual_schedule())
 
+        grad_raw = []
+
+        def load_grad(c):
+            g_raw = keep.tile([P, LOAD_TILES, OUT_FEATURES], BF16, name="g_raw%d" % c)
+            nc.sync.dma_start(out=g_raw[:], in_=grad_by_tile[:, c * LOAD_TILES : (c + 1) * LOAD_TILES, :])
+            grad_raw.append(g_raw)
+
+        load_grad(0)
         weight_raw, mask_raw = [], []
         for u in range(2):
             rows = slice(u * K_HALF, (u + 1) * K_HALF)
@@ -50,37 +58,38 @@ def tile_structuredconnection_t_kernel(tc, x, weight, bias, mask, grad_out, out)
             nc.sync.dma_start(out=m_raw[:], in_=mask[rows, :].rearrange("(p e) c -> p e c", e=2))
             weight_raw.append(w_raw)
             mask_raw.append(m_raw)
-        grad_raw = []
-        for c in range(N_LOADS):
-            g_raw = keep.tile([P, LOAD_TILES, OUT_FEATURES], BF16, name="g_raw%d" % c)
-            nc.sync.dma_start(out=g_raw[:], in_=grad_by_tile[:, c * LOAD_TILES : (c + 1) * LOAD_TILES, :])
-            grad_raw.append(g_raw)
+        for c in range(1, N_LOADS):
+            load_grad(c)
 
         identity = keep.tile([P, P], F32, name="identity")
         make_identity(nc, identity[:])
 
         masked = keep.tile([P, PACK, IN_FEATURES], BF16, name="masked")
-        for u in range(2):
-            nc.vector.tensor_tensor(
-                out=masked[:, 2 * u : 2 * u + 2, :],
-                in0=weight_raw[u][:],
-                in1=mask_raw[u][:],
-                op=mybir.AluOpType.mult,
-            )
         w_grouped = keep.tile([P, IN_FEATURES, PACK], BF16, name="w_grouped", align_bytes=64)
         w_codes = keep.tile([P, IN_FEATURES], U32, name="w_codes", align_bytes=64)
         w_scales = keep.tile([P, IN_FEATURES], U8, name="w_scales", align_bytes=64)
         column_halves = [slice(h * N_PASS, (h + 1) * N_PASS) for h in range(COLUMN_HALVES)]
-        for cols in column_halves:
-            nc.vector.tensor_copy(
-                out=w_grouped[:, cols, :], in_=masked[:, :, cols].rearrange("p t c -> p c t")
-            )
-        for cols in column_halves:
-            nc.vector.quantize_mx(
-                out=w_codes[:, cols].bitcast(E4M3_X4),
-                scales=w_scales[:, cols],
-                in_=w_grouped[:, cols, :].rearrange("p c t -> p (c t)"),
-            )
+
+        def prepare_weights():
+            for u in range(2):
+                nc.vector.tensor_tensor(
+                    out=masked[:, 2 * u : 2 * u + 2, :],
+                    in0=weight_raw[u][:],
+                    in1=mask_raw[u][:],
+                    op=mybir.AluOpType.mult,
+                )
+            for h, cols in enumerate(column_halves):
+                four_rows_alternately = masked[:, :, cols].rearrange("p t c -> p c t")
+                if h == 0:
+                    nc.vector.tensor_copy(out=w_grouped[:, cols, :], in_=four_rows_alternately)
+                else:
+                    nc.scalar.copy(out=w_grouped[:, cols, :], in_=four_rows_alternately)
+            for cols in column_halves:
+                nc.vector.quantize_mx(
+                    out=w_codes[:, cols].bitcast(E4M3_X4),
+                    scales=w_scales[:, cols],
+                    in_=w_grouped[:, cols, :].rearrange("p c t -> p (c t)"),
+                )
 
         def transpose_group(g):
             flipped = flipped_banks.tile([P, GROUP, 2, P], F32, name="flipped")
@@ -105,9 +114,9 @@ def tile_structuredconnection_t_kernel(tc, x, weight, bias, mask, grad_out, out)
 
         def multiply_group(g, g_codes, g_scales):
             result = results.tile([P, GROUP, IN_FEATURES], F32, name="result")
-            for a in range(GROUP):
-                tokens = slice(a * P, (a + 1) * P)
-                for h, cols in enumerate(column_halves):
+            for h, cols in enumerate(column_halves):
+                for a in range(GROUP):
+                    tokens = slice(a * P, (a + 1) * P)
                     product = product_banks.tile([P, N_PASS], F32, name="product")
                     nc.tensor.matmul_mx(
                         out=product[:],
@@ -126,6 +135,7 @@ def tile_structuredconnection_t_kernel(tc, x, weight, bias, mask, grad_out, out)
 
         grouped = {0: transpose_group(0), 1: transpose_group(1)}
         quantised = {0: quantise_group(grouped[0])}
+        prepare_weights()
         for g in range(N_GROUPS):
             if g + 2 < N_GROUPS:
                 grouped[g + 2] = transpose_group(g + 2)

@@ -24,7 +24,9 @@ COLUMN_HALVES = IN_FEATURES // N_PASS
 TOKEN_TILES = TOKENS // P
 GROUP = 2
 N_GROUPS = TOKEN_TILES // GROUP
-LOAD_TILES = 4
+SPLIT_GROUPS = 2
+RUN = 4
+LOAD_TILES = 8
 N_LOADS = TOKEN_TILES // LOAD_TILES
 
 
@@ -41,14 +43,6 @@ def tile_structuredconnection_t_kernel(tc, x, weight, bias, mask, grad_out, out)
         product_banks = stack.enter_context(tc.psum_pool(name="product_banks", bufs=6))
         stack.enter_context(tc.manual_schedule())
 
-        grad_raw = []
-
-        def load_grad(c):
-            g_raw = keep.tile([P, LOAD_TILES, OUT_FEATURES], BF16, name="g_raw%d" % c)
-            nc.sync.dma_start(out=g_raw[:], in_=grad_by_tile[:, c * LOAD_TILES : (c + 1) * LOAD_TILES, :])
-            grad_raw.append(g_raw)
-
-        load_grad(0)
         weight_raw, mask_raw = [], []
         for u in range(2):
             rows = slice(u * K_HALF, (u + 1) * K_HALF)
@@ -58,38 +52,40 @@ def tile_structuredconnection_t_kernel(tc, x, weight, bias, mask, grad_out, out)
             nc.sync.dma_start(out=m_raw[:], in_=mask[rows, :].rearrange("(p e) c -> p e c", e=2))
             weight_raw.append(w_raw)
             mask_raw.append(m_raw)
-        for c in range(1, N_LOADS):
-            load_grad(c)
+        grad_raw = []
+        for c in range(N_LOADS):
+            g_raw = keep.tile([P, LOAD_TILES, OUT_FEATURES], BF16, name="g_raw%d" % c)
+            nc.sync.dma_start(out=g_raw[:], in_=grad_by_tile[:, c * LOAD_TILES : (c + 1) * LOAD_TILES, :])
+            grad_raw.append(g_raw)
 
         identity = keep.tile([P, P], F32, name="identity")
         make_identity(nc, identity[:])
 
         masked = keep.tile([P, PACK, IN_FEATURES], BF16, name="masked")
+        for u in range(2):
+            nc.vector.tensor_tensor(
+                out=masked[:, 2 * u : 2 * u + 2, :],
+                in0=weight_raw[u][:],
+                in1=mask_raw[u][:],
+                op=mybir.AluOpType.mult,
+            )
         w_grouped = keep.tile([P, IN_FEATURES, PACK], BF16, name="w_grouped", align_bytes=64)
         w_codes = keep.tile([P, IN_FEATURES], U32, name="w_codes", align_bytes=64)
         w_scales = keep.tile([P, IN_FEATURES], U8, name="w_scales", align_bytes=64)
         column_halves = [slice(h * N_PASS, (h + 1) * N_PASS) for h in range(COLUMN_HALVES)]
-
-        def prepare_weights():
-            for u in range(2):
-                nc.vector.tensor_tensor(
-                    out=masked[:, 2 * u : 2 * u + 2, :],
-                    in0=weight_raw[u][:],
-                    in1=mask_raw[u][:],
-                    op=mybir.AluOpType.mult,
-                )
-            for h, cols in enumerate(column_halves):
-                four_rows_alternately = masked[:, :, cols].rearrange("p t c -> p c t")
-                if h == 0:
-                    nc.vector.tensor_copy(out=w_grouped[:, cols, :], in_=four_rows_alternately)
-                else:
-                    nc.scalar.copy(out=w_grouped[:, cols, :], in_=four_rows_alternately)
-            for cols in column_halves:
-                nc.vector.quantize_mx(
-                    out=w_codes[:, cols].bitcast(E4M3_X4),
-                    scales=w_scales[:, cols],
-                    in_=w_grouped[:, cols, :].rearrange("p c t -> p (c t)"),
-                )
+        for h, cols in enumerate(column_halves):
+            side_by_side = w_grouped[:, cols, :].rearrange("p (c i) t -> p c t i", i=RUN)
+            row_by_row = masked[:, :, cols].rearrange("p t (c i) -> p c t i", i=RUN)
+            if h == 0:
+                nc.vector.tensor_copy(out=side_by_side, in_=row_by_row)
+            else:
+                nc.scalar.copy(out=side_by_side, in_=row_by_row)
+        for cols in column_halves:
+            nc.vector.quantize_mx(
+                out=w_codes[:, cols].bitcast(E4M3_X4),
+                scales=w_scales[:, cols],
+                in_=w_grouped[:, cols, :].rearrange("p c t -> p (c t)"),
+            )
 
         def transpose_group(g):
             flipped = flipped_banks.tile([P, GROUP, 2, P], F32, name="flipped")
@@ -114,9 +110,9 @@ def tile_structuredconnection_t_kernel(tc, x, weight, bias, mask, grad_out, out)
 
         def multiply_group(g, g_codes, g_scales):
             result = results.tile([P, GROUP, IN_FEATURES], F32, name="result")
-            for h, cols in enumerate(column_halves):
-                for a in range(GROUP):
-                    tokens = slice(a * P, (a + 1) * P)
+            for a in range(GROUP):
+                tokens = slice(a * P, (a + 1) * P)
+                for h, cols in enumerate(column_halves):
                     product = product_banks.tile([P, N_PASS], F32, name="product")
                     nc.tensor.matmul_mx(
                         out=product[:],
@@ -131,11 +127,13 @@ def tile_structuredconnection_t_kernel(tc, x, weight, bias, mask, grad_out, out)
                         nc.scalar.copy(out=result[:, a, cols], in_=product[:])
                     else:
                         nc.vector.tensor_copy(out=result[:, a, cols], in_=product[:])
-            nc.sync.dma_start(out=out_by_tile[:, g * GROUP : (g + 1) * GROUP, :], in_=result[:])
+                if g < SPLIT_GROUPS:
+                    nc.sync.dma_start(out=out_by_tile[:, g * GROUP + a, :], in_=result[:, a, :])
+            if g >= SPLIT_GROUPS:
+                nc.sync.dma_start(out=out_by_tile[:, g * GROUP : (g + 1) * GROUP, :], in_=result[:])
 
         grouped = {0: transpose_group(0), 1: transpose_group(1)}
         quantised = {0: quantise_group(grouped[0])}
-        prepare_weights()
         for g in range(N_GROUPS):
             if g + 2 < N_GROUPS:
                 grouped[g + 2] = transpose_group(g + 2)

@@ -132,7 +132,20 @@ def tile_structuredconnection_t_kernel(tc, x, weight, bias, mask, grad_out, out)
             if g >= SPLIT_GROUPS:
                 nc.sync.dma_start(out=out_by_tile[:, g * GROUP : (g + 1) * GROUP, :], in_=result[:])
 
+        def keep_tensor_busy(count):
+            unread = product_banks.tile([P, N_PASS], F32, name="product")
+            for step in range(count):
+                nc.tensor.matmul(
+                    unread[:],
+                    lhsT=mask_raw[0][:, 0, :P],
+                    rhs=mask_raw[0][:, 1, :N_PASS],
+                    start=True,
+                    stop=True,
+                )
+
+        keep_tensor_busy(6)
         grouped = {0: transpose_group(0), 1: transpose_group(1)}
+        keep_tensor_busy(4)
         quantised = {0: quantise_group(grouped[0])}
         for g in range(N_GROUPS):
             if g + 2 < N_GROUPS:

@@ -73,14 +73,17 @@ def tile_structuredconnection_t_kernel(tc, x, weight, bias, mask, grad_out, out)
         w_codes = keep.tile([P, IN_FEATURES], U32, name="w_codes", align_bytes=64)
         w_scales = keep.tile([P, IN_FEATURES], U8, name="w_scales", align_bytes=64)
         column_halves = [slice(h * N_PASS, (h + 1) * N_PASS) for h in range(COLUMN_HALVES)]
-        for h, cols in enumerate(column_halves):
-            side_by_side = w_grouped[:, cols, :].rearrange("p (c i) t -> p c t i", i=RUN)
-            row_by_row = masked[:, :, cols].rearrange("p t (c i) -> p c t i", i=RUN)
-            if h == 0:
-                nc.vector.tensor_copy(out=side_by_side, in_=row_by_row)
-            else:
-                nc.scalar.copy(out=side_by_side, in_=row_by_row)
-        for cols in column_halves:
+        for first, last, copy in (
+            (0, N_PASS, nc.vector.tensor_copy),
+            (N_PASS, IN_FEATURES - N_PASS // 2, nc.vector.tensor_copy),
+            (IN_FEATURES - N_PASS // 2, IN_FEATURES, nc.scalar.copy),
+        ):
+            copy(
+                out=w_grouped[:, first:last, :].rearrange("p (c i) t -> p c t i", i=RUN),
+                in_=masked[:, :, first:last].rearrange("p t (c i) -> p c t i", i=RUN),
+            )
+
+        def quantise_weights(cols):
             nc.vector.quantize_mx(
                 out=w_codes[:, cols].bitcast(E4M3_X4),
                 scales=w_scales[:, cols],
@@ -146,7 +149,9 @@ def tile_structuredconnection_t_kernel(tc, x, weight, bias, mask, grad_out, out)
         keep_tensor_busy(6)
         grouped = {0: transpose_group(0), 1: transpose_group(1)}
         keep_tensor_busy(4)
+        quantise_weights(column_halves[0])
         quantised = {0: quantise_group(grouped[0])}
+        quantise_weights(column_halves[1])
         for g in range(N_GROUPS):
             if g + 2 < N_GROUPS:
                 grouped[g + 2] = transpose_group(g + 2)

@@ -24,10 +24,10 @@ COLUMN_HALVES = IN_FEATURES // N_PASS
 TOKEN_TILES = TOKENS // P
 GROUP = 2
 N_GROUPS = TOKEN_TILES // GROUP
-SPLIT_GROUPS = 2
+SINGLE_STORES = 4
+PAIR_STORES = 4
 RUN = 4
-LOAD_TILES = 8
-N_LOADS = TOKEN_TILES // LOAD_TILES
+LOAD_STARTS = (0, 8, 16)
 
 
 def tile_structuredconnection_t_kernel(tc, x, weight, bias, mask, grad_out, out):
@@ -38,7 +38,7 @@ def tile_structuredconnection_t_kernel(tc, x, weight, bias, mask, grad_out, out)
     with ExitStack() as stack:
         keep = stack.enter_context(tc.tile_pool(name="keep", bufs=1))
         stage = stack.enter_context(tc.tile_pool(name="stage", bufs=3))
-        results = stack.enter_context(tc.tile_pool(name="results", bufs=4))
+        results = stack.enter_context(tc.tile_pool(name="results", bufs=1))
         flipped_banks = stack.enter_context(tc.psum_pool(name="flipped_banks", bufs=2))
         product_banks = stack.enter_context(tc.psum_pool(name="product_banks", bufs=6))
         stack.enter_context(tc.manual_schedule())
@@ -53,10 +53,10 @@ def tile_structuredconnection_t_kernel(tc, x, weight, bias, mask, grad_out, out)
             weight_raw.append(w_raw)
             mask_raw.append(m_raw)
         grad_raw = []
-        for c in range(N_LOADS):
-            g_raw = keep.tile([P, LOAD_TILES, OUT_FEATURES], BF16, name="g_raw%d" % c)
-            nc.sync.dma_start(out=g_raw[:], in_=grad_by_tile[:, c * LOAD_TILES : (c + 1) * LOAD_TILES, :])
-            grad_raw.append(g_raw)
+        for first, last in zip(LOAD_STARTS, LOAD_STARTS[1:] + (TOKEN_TILES,)):
+            g_raw = keep.tile([P, last - first, OUT_FEATURES], BF16, name="g_raw%d" % first)
+            nc.sync.dma_start(out=g_raw[:], in_=grad_by_tile[:, first:last, :])
+            grad_raw.extend(g_raw[:, t, :] for t in range(last - first))
 
         identity = keep.tile([P, P], F32, name="identity")
         make_identity(nc, identity[:])
@@ -90,11 +90,23 @@ def tile_structuredconnection_t_kernel(tc, x, weight, bias, mask, grad_out, out)
                 in_=w_grouped[:, cols, :].rearrange("p c t -> p (c t)"),
             )
 
+        store_of = []
+        while len(store_of) < TOKEN_TILES:
+            first = len(store_of)
+            if first < SINGLE_STORES:
+                width = 1
+            elif first < SINGLE_STORES + 2 * PAIR_STORES:
+                width = 2
+            else:
+                width = 4
+            result = results.tile([P, width, IN_FEATURES], F32, name="result%d" % first)
+            store_of.extend((first, first + width, result) for t in range(width))
+
         def transpose_group(g):
             flipped = flipped_banks.tile([P, GROUP, 2, P], F32, name="flipped")
             for a in range(GROUP):
                 t = g * GROUP + a
-                words = grad_raw[t // LOAD_TILES][:].bitcast(F32)[:, t % LOAD_TILES, :]
+                words = grad_raw[t].bitcast(F32)
                 for u in range(2):
                     nc.tensor.transpose(flipped[:, a, u, :], words[:, u * P : (u + 1) * P], identity[:])
             g_grouped = stage.tile([P, GROUP, P, PACK], BF16, name="g_grouped", align_bytes=64)
@@ -112,8 +124,9 @@ def tile_structuredconnection_t_kernel(tc, x, weight, bias, mask, grad_out, out)
             return g_codes, g_scales
 
         def multiply_group(g, g_codes, g_scales):
-            result = results.tile([P, GROUP, IN_FEATURES], F32, name="result")
             for a in range(GROUP):
+                t = g * GROUP + a
+                first, last, result = store_of[t]
                 tokens = slice(a * P, (a + 1) * P)
                 for h, cols in enumerate(column_halves):
                     product = product_banks.tile([P, N_PASS], F32, name="product")
@@ -127,13 +140,11 @@ def tile_structuredconnection_t_kernel(tc, x, weight, bias, mask, grad_out, out)
                         stop=True,
                     )
                     if h == 0:
-                        nc.scalar.copy(out=result[:, a, cols], in_=product[:])
+                        nc.scalar.copy(out=result[:, t - first, cols], in_=product[:])
                     else:
-                        nc.vector.tensor_copy(out=result[:, a, cols], in_=product[:])
-                if g < SPLIT_GROUPS:
-                    nc.sync.dma_start(out=out_by_tile[:, g * GROUP + a, :], in_=result[:, a, :])
-            if g >= SPLIT_GROUPS:
-                nc.sync.dma_start(out=out_by_tile[:, g * GROUP : (g + 1) * GROUP, :], in_=result[:])
+                        nc.vector.tensor_copy(out=result[:, t - first, cols], in_=product[:])
+                if t == last - 1:
+                    nc.sync.dma_start(out=out_by_tile[:, first:last, :], in_=result[:])
 
         def keep_tensor_busy(count):
             unread = product_banks.tile([P, N_PASS], F32, name="product")

@@ -27,7 +27,8 @@ N_GROUPS = TOKEN_TILES // GROUP
 SINGLE_STORES = 4
 PAIR_STORES = 4
 RUN = 4
-LOAD_STARTS = (0, 8, 16)
+LOAD_STARTS = (0, 4, 8, 16)
+SCALAR_COLUMNS = 3 * IN_FEATURES // 8
 
 
 def tile_structuredconnection_t_kernel(tc, x, weight, bias, mask, grad_out, out):
@@ -61,26 +62,33 @@ def tile_structuredconnection_t_kernel(tc, x, weight, bias, mask, grad_out, out)
         identity = keep.tile([P, P], F32, name="identity")
         make_identity(nc, identity[:])
 
-        masked = keep.tile([P, PACK, IN_FEATURES], BF16, name="masked")
+        vector_columns = IN_FEATURES - SCALAR_COLUMNS
+        masked_scalar = keep.tile([P, PACK, SCALAR_COLUMNS], BF16, name="masked_scalar")
+        masked_vector = keep.tile([P, PACK, vector_columns], BF16, name="masked_vector")
         for u in range(2):
-            nc.vector.tensor_tensor(
-                out=masked[:, 2 * u : 2 * u + 2, :],
-                in0=weight_raw[u][:],
-                in1=mask_raw[u][:],
-                op=mybir.AluOpType.mult,
-            )
+            for masked, first, last in (
+                (masked_scalar, vector_columns, IN_FEATURES),
+                (masked_vector, 0, vector_columns),
+            ):
+                nc.vector.tensor_tensor(
+                    out=masked[:, 2 * u : 2 * u + 2, :],
+                    in0=weight_raw[u][:, :, first:last],
+                    in1=mask_raw[u][:, :, first:last],
+                    op=mybir.AluOpType.mult,
+                )
         w_grouped = keep.tile([P, IN_FEATURES, PACK], BF16, name="w_grouped", align_bytes=64)
         w_codes = keep.tile([P, IN_FEATURES], U32, name="w_codes", align_bytes=64)
         w_scales = keep.tile([P, IN_FEATURES], U8, name="w_scales", align_bytes=64)
         column_halves = [slice(h * N_PASS, (h + 1) * N_PASS) for h in range(COLUMN_HALVES)]
-        for first, last, copy in (
-            (0, N_PASS, nc.vector.tensor_copy),
-            (N_PASS, IN_FEATURES - N_PASS // 2, nc.vector.tensor_copy),
-            (IN_FEATURES - N_PASS // 2, IN_FEATURES, nc.scalar.copy),
+        for copy, masked, first, last in (
+            (nc.vector.tensor_copy, masked_vector, 0, N_PASS),
+            (nc.vector.tensor_copy, masked_vector, N_PASS, vector_columns),
+            (nc.scalar.copy, masked_scalar, vector_columns, IN_FEATURES),
         ):
+            offset = 0 if masked is masked_vector else vector_columns
             copy(
                 out=w_grouped[:, first:last, :].rearrange("p (c i) t -> p c t i", i=RUN),
-                in_=masked[:, :, first:last].rearrange("p t (c i) -> p c t i", i=RUN),
+                in_=masked[:, :, first - offset : last - offset].rearrange("p t (c i) -> p c t i", i=RUN),
             )
 
         def quantise_weights(cols):
@@ -146,20 +154,21 @@ def tile_structuredconnection_t_kernel(tc, x, weight, bias, mask, grad_out, out)
                 if t == last - 1:
                     nc.sync.dma_start(out=out_by_tile[:, first:last, :], in_=result[:])
 
-        def keep_tensor_busy(count):
+        def keep_tensor_busy(ones, count):
             unread = product_banks.tile([P, N_PASS], F32, name="product")
             for step in range(count):
                 nc.tensor.matmul(
                     unread[:],
-                    lhsT=mask_raw[0][:, 0, :P],
-                    rhs=mask_raw[0][:, 1, :N_PASS],
+                    lhsT=ones[:, 0, :P],
+                    rhs=ones[:, 1, :N_PASS],
                     start=True,
                     stop=True,
                 )
 
-        keep_tensor_busy(6)
+        keep_tensor_busy(mask_raw[0], 6)
+        keep_tensor_busy(mask_raw[1], 4)
         grouped = {0: transpose_group(0), 1: transpose_group(1)}
-        keep_tensor_busy(4)
+        keep_tensor_busy(mask_raw[1], 5)
         quantise_weights(column_halves[0])
         quantised = {0: quantise_group(grouped[0])}
         quantise_weights(column_halves[1])

@@ -21,6 +21,8 @@ K_HALF = OUT_FEATURES // 2
 N_PASS = 512
 COLUMN_HALVES = IN_FEATURES // N_PASS
 
+DMA_ALIGN = 256
+
 TOKEN_TILES = TOKENS // P
 GROUP = 2
 N_GROUPS = TOKEN_TILES // GROUP
@@ -47,15 +49,15 @@ def tile_structuredconnection_t_kernel(tc, x, weight, bias, mask, grad_out, out)
         weight_raw, mask_raw = [], []
         for u in range(2):
             rows = slice(u * K_HALF, (u + 1) * K_HALF)
-            w_raw = keep.tile([P, 2, IN_FEATURES], BF16, name="w_raw%d" % u)
-            m_raw = keep.tile([P, 2, IN_FEATURES], BF16, name="m_raw%d" % u)
+            w_raw = keep.tile([P, 2, IN_FEATURES], BF16, name="w_raw%d" % u, align_bytes=DMA_ALIGN)
+            m_raw = keep.tile([P, 2, IN_FEATURES], BF16, name="m_raw%d" % u, align_bytes=DMA_ALIGN)
             nc.sync.dma_start(out=w_raw[:], in_=weight[rows, :].rearrange("(p e) c -> p e c", e=2))
             nc.sync.dma_start(out=m_raw[:], in_=mask[rows, :].rearrange("(p e) c -> p e c", e=2))
             weight_raw.append(w_raw)
             mask_raw.append(m_raw)
         grad_raw = []
         for first, last in zip(LOAD_STARTS, LOAD_STARTS[1:] + (TOKEN_TILES,)):
-            g_raw = keep.tile([P, last - first, OUT_FEATURES], BF16, name="g_raw%d" % first)
+            g_raw = keep.tile([P, last - first, OUT_FEATURES], BF16, name="g_raw%d" % first, align_bytes=DMA_ALIGN)
             nc.sync.dma_start(out=g_raw[:], in_=grad_by_tile[:, first:last, :])
             grad_raw.extend(g_raw[:, t, :] for t in range(last - first))
 
@@ -107,7 +109,7 @@ def tile_structuredconnection_t_kernel(tc, x, weight, bias, mask, grad_out, out)
                 width = 2
             else:
                 width = 4
-            result = results.tile([P, width, IN_FEATURES], F32, name="result%d" % first)
+            result = results.tile([P, width, IN_FEATURES], F32, name="result%d" % first, align_bytes=DMA_ALIGN)
             store_of.extend((first, first + width, result) for t in range(width))
 
         def transpose_group(g):

@@ -21,7 +21,7 @@ K_HALF = OUT_FEATURES // 2
 N_PASS = 512
 COLUMN_HALVES = IN_FEATURES // N_PASS
 
-DMA_ALIGN = 256
+DMA_ALIGN = 4096
 
 TOKEN_TILES = TOKENS // P
 GROUP = 2
@@ -55,11 +55,9 @@ def tile_structuredconnection_t_kernel(tc, x, weight, bias, mask, grad_out, out)
             nc.sync.dma_start(out=m_raw[:], in_=mask[rows, :].rearrange("(p e) c -> p e c", e=2))
             weight_raw.append(w_raw)
             mask_raw.append(m_raw)
-        grad_raw = []
+        g_raw = keep.tile([P, TOKEN_TILES, OUT_FEATURES], BF16, name="g_raw", align_bytes=DMA_ALIGN)
         for first, last in zip(LOAD_STARTS, LOAD_STARTS[1:] + (TOKEN_TILES,)):
-            g_raw = keep.tile([P, last - first, OUT_FEATURES], BF16, name="g_raw%d" % first, align_bytes=DMA_ALIGN)
-            nc.sync.dma_start(out=g_raw[:], in_=grad_by_tile[:, first:last, :])
-            grad_raw.extend(g_raw[:, t, :] for t in range(last - first))
+            nc.sync.dma_start(out=g_raw[:, first:last, :], in_=grad_by_tile[:, first:last, :])
 
         identity = keep.tile([P, P], F32, name="identity")
         make_identity(nc, identity[:])
@@ -100,6 +98,7 @@ def tile_structuredconnection_t_kernel(tc, x, weight, bias, mask, grad_out, out)
                 in_=w_grouped[:, cols, :].rearrange("p c t -> p (c t)"),
             )
 
+        result = results.tile([P, TOKEN_TILES, IN_FEATURES], F32, name="result", align_bytes=DMA_ALIGN)
         store_of = []
         while len(store_of) < TOKEN_TILES:
             first = len(store_of)
@@ -109,14 +108,13 @@ def tile_structuredconnection_t_kernel(tc, x, weight, bias, mask, grad_out, out)
                 width = 2
             else:
                 width = 4
-            result = results.tile([P, width, IN_FEATURES], F32, name="result%d" % first, align_bytes=DMA_ALIGN)
-            store_of.extend((first, first + width, result) for t in range(width))
+            store_of.extend((first, first + width) for t in range(width))
 
         def transpose_group(g):
             flipped = flipped_banks.tile([P, GROUP, 2, P], F32, name="flipped")
             for a in range(GROUP):
                 t = g * GROUP + a
-                words = grad_raw[t].bitcast(F32)
+                words = g_raw[:, t, :].bitcast(F32)
                 for u in range(2):
                     nc.tensor.transpose(flipped[:, a, u, :], words[:, u * P : (u + 1) * P], identity[:])
             g_grouped = stage.tile([P, GROUP, P, PACK], BF16, name="g_grouped", align_bytes=64)
@@ -136,7 +134,7 @@ def tile_structuredconnection_t_kernel(tc, x, weight, bias, mask, grad_out, out)
         def multiply_group(g, g_codes, g_scales):
             for a in range(GROUP):
                 t = g * GROUP + a
-                first, last, result = store_of[t]
+                first, last = store_of[t]
                 tokens = slice(a * P, (a + 1) * P)
                 for h, cols in enumerate(column_halves):
                     product = product_banks.tile([P, N_PASS], F32, name="product")
@@ -150,11 +148,11 @@ def tile_structuredconnection_t_kernel(tc, x, weight, bias, mask, grad_out, out)
                         stop=True,
                     )
                     if h == 0:
-                        nc.scalar.copy(out=result[:, t - first, cols], in_=product[:])
+                        nc.scalar.copy(out=result[:, t, cols], in_=product[:])
                     else:
-                        nc.vector.tensor_copy(out=result[:, t - first, cols], in_=product[:])
+                        nc.vector.tensor_copy(out=result[:, t, cols], in_=product[:])
                 if t == last - 1:
-                    nc.sync.dma_start(out=out_by_tile[:, first:last, :], in_=result[:])
+                    nc.sync.dma_start(out=out_by_tile[:, first:last, :], in_=result[:, first:last, :])
 
         def keep_tensor_busy(ones, count):
             unread = product_banks.tile([P, N_PASS], F32, name="product")

from contextlib import ExitStack

import concourse.mybir as mybir
from concourse.masks import make_identity

BF16 = mybir.dt.bfloat16
F32 = mybir.dt.float32
U32 = mybir.dt.uint32
U8 = mybir.dt.uint8
E4M3_X4 = mybir.dt.float8_e4m3fn_x4
E5M2_X4 = mybir.dt.float8_e5m2_x4

TOKENS, IN_FEATURES, OUT_FEATURES = 4096, 1024, 512
FLOPS = 2 * TOKENS * IN_FEATURES * OUT_FEATURES
BYTES = 2 * (TOKENS * OUT_FEATURES + 2 * OUT_FEATURES * IN_FEATURES) + 4 * TOKENS * IN_FEATURES

P = 128
PACK = 4
assert OUT_FEATURES == P * PACK
K_HALF = OUT_FEATURES // 2
N_PASS = 512
COLUMN_HALVES = IN_FEATURES // N_PASS

DMA_ALIGN = 4096

TOKEN_TILES = TOKENS // P
GROUP = 2
N_GROUPS = TOKEN_TILES // GROUP
SINGLE_STORES = 4
PAIR_STORES = 4
RUN = 4
LOAD_STARTS = (0, 4, 8, 16)
SCALAR_COLUMNS = 3 * IN_FEATURES // 8


def tile_structuredconnection_t_kernel(tc, x, weight, bias, mask, grad_out, out):
    nc = tc.nc
    grad_by_tile = grad_out.rearrange("(p t) k -> p t k", t=TOKEN_TILES)
    out_by_tile = out.rearrange("(p t) i -> p t i", t=TOKEN_TILES)

    with ExitStack() as stack:
        keep = stack.enter_context(tc.tile_pool(name="keep", bufs=1))
        stage = stack.enter_context(tc.tile_pool(name="stage", bufs=3))
        results = stack.enter_context(tc.tile_pool(name="results", bufs=1))
        flipped_banks = stack.enter_context(tc.psum_pool(name="flipped_banks", bufs=2))
        product_banks = stack.enter_context(tc.psum_pool(name="product_banks", bufs=6))
        stack.enter_context(tc.manual_schedule())

        weight_raw, mask_raw = [], []
        for u in range(2):
            rows = slice(u * K_HALF, (u + 1) * K_HALF)
            w_raw = keep.tile([P, 2, IN_FEATURES], BF16, name="w_raw%d" % u, align_bytes=DMA_ALIGN)
            m_raw = keep.tile([P, 2, IN_FEATURES], BF16, name="m_raw%d" % u, align_bytes=DMA_ALIGN)
            nc.sync.dma_start(out=w_raw[:], in_=weight[rows, :].rearrange("(p e) c -> p e c", e=2))
            nc.sync.dma_start(out=m_raw[:], in_=mask[rows, :].rearrange("(p e) c -> p e c", e=2))
            weight_raw.append(w_raw)
            mask_raw.append(m_raw)
        g_raw = keep.tile([P, TOKEN_TILES, OUT_FEATURES], BF16, name="g_raw", align_bytes=DMA_ALIGN)
        for first, last in zip(LOAD_STARTS, LOAD_STARTS[1:] + (TOKEN_TILES,)):
            nc.sync.dma_start(out=g_raw[:, first:last, :], in_=grad_by_tile[:, first:last, :])

        identity = keep.tile([P, P], F32, name="identity")
        make_identity(nc, identity[:])

        vector_columns = IN_FEATURES - SCALAR_COLUMNS
        masked_scalar = keep.tile([P, PACK, SCALAR_COLUMNS], BF16, name="masked_scalar")
        masked_vector = keep.tile([P, PACK, vector_columns], BF16, name="masked_vector")
        for u in range(2):
            for masked, first, last in (
                (masked_scalar, vector_columns, IN_FEATURES),
                (masked_vector, 0, vector_columns),
            ):
                nc.vector.tensor_tensor(
                    out=masked[:, 2 * u : 2 * u + 2, :],
                    in0=weight_raw[u][:, :, first:last],
                    in1=mask_raw[u][:, :, first:last],
                    op=mybir.AluOpType.mult,
                )
        w_grouped = keep.tile([P, IN_FEATURES, PACK], BF16, name="w_grouped", align_bytes=64)
        w_codes = keep.tile([P, IN_FEATURES], U32, name="w_codes", align_bytes=64)
        w_scales = keep.tile([P, IN_FEATURES], U8, name="w_scales", align_bytes=64)
        column_halves = [slice(h * N_PASS, (h + 1) * N_PASS) for h in range(COLUMN_HALVES)]
        for copy, masked, first, last in (
            (nc.vector.tensor_copy, masked_vector, 0, N_PASS),
            (nc.vector.tensor_copy, masked_vector, N_PASS, vector_columns),
            (nc.scalar.copy, masked_scalar, vector_columns, IN_FEATURES),
        ):
            offset = 0 if masked is masked_vector else vector_columns
            copy(
                out=w_grouped[:, first:last, :].rearrange("p (c i) t -> p c t i", i=RUN),
                in_=masked[:, :, first - offset : last - offset].rearrange("p t (c i) -> p c t i", i=RUN),
            )

        def quantise_weights(cols):
            nc.vector.quantize_mx(
                out=w_codes[:, cols].bitcast(E4M3_X4),
                scales=w_scales[:, cols],
                in_=w_grouped[:, cols, :].rearrange("p c t -> p (c t)"),
            )

        result = results.tile([P, TOKEN_TILES, IN_FEATURES], F32, name="result", align_bytes=DMA_ALIGN)
        store_of = []
        while len(store_of) < TOKEN_TILES:
            first = len(store_of)
            if first < SINGLE_STORES:
                width = 1
            elif first < SINGLE_STORES + 2 * PAIR_STORES:
                width = 2
            else:
                width = 4
            store_of.extend((first, first + width) for t in range(width))

        def transpose_group(g):
            flipped = flipped_banks.tile([P, GROUP, 2, P], F32, name="flipped")
            for a in range(GROUP):
                t = g * GROUP + a
                words = g_raw[:, t, :].bitcast(F32)
                for u in range(2):
                    nc.tensor.transpose(flipped[:, a, u, :], words[:, u * P : (u + 1) * P], identity[:])
            g_grouped = stage.tile([P, GROUP, P, PACK], BF16, name="g_grouped", align_bytes=64)
            nc.scalar.copy(out=g_grouped[:].bitcast(F32), in_=flipped[:].rearrange("p a u r -> p a r u"))
            return g_grouped

        def quantise_group(g_grouped):
            g_codes = stage.tile([P, GROUP * P], U32, name="g_codes", align_bytes=64)
            g_scales = stage.tile([P, GROUP * P], U8, name="g_scales", align_bytes=64)
            nc.vector.quantize_mx(
                out=g_codes[:].bitcast(E5M2_X4),
                scales=g_scales[:],
                in_=g_grouped[:].rearrange("p a r t -> p (a r t)"),
            )
            return g_codes, g_scales

        def multiply_group(g, g_codes, g_scales):
            for a in range(GROUP):
                t = g * GROUP + a
                first, last = store_of[t]
                tokens = slice(a * P, (a + 1) * P)
                for h, cols in enumerate(column_halves):
                    product = product_banks.tile([P, N_PASS], F32, name="product")
                    nc.tensor.matmul_mx(
                        out=product[:],
                        lhsT=g_codes[:, tokens].bitcast(E5M2_X4),
                        lhsT_scale=g_scales[:, tokens],
                        rhs=w_codes[:, cols].bitcast(E4M3_X4),
                        rhs_scale=w_scales[:, cols],
                        start=True,
                        stop=True,
                    )
                    if h == 0:
                        nc.scalar.copy(out=result[:, t, cols], in_=product[:])
                    else:
                        nc.vector.tensor_copy(out=result[:, t, cols], in_=product[:])
                if t == last - 1:
                    nc.sync.dma_start(out=out_by_tile[:, first:last, :], in_=result[:, first:last, :])

        def keep_tensor_busy(ones, count):
            unread = product_banks.tile([P, N_PASS], F32, name="product")
            for step in range(count):
                nc.tensor.matmul(
                    unread[:],
                    lhsT=ones[:, 0, :P],
                    rhs=ones[:, 1, :N_PASS],
                    start=True,
                    stop=True,
                )

        keep_tensor_busy(mask_raw[0], 6)
        keep_tensor_busy(mask_raw[1], 4)
        grouped = {0: transpose_group(0), 1: transpose_group(1)}
        keep_tensor_busy(mask_raw[1], 5)
        quantise_weights(column_halves[0])
        quantised = {0: quantise_group(grouped[0])}
        quantise_weights(column_halves[1])
        for g in range(N_GROUPS):
            if g + 2 < N_GROUPS:
                grouped[g + 2] = transpose_group(g + 2)
            if g + 1 < N_GROUPS:
                quantised[g + 1] = quantise_group(grouped[g + 1])
            multiply_group(g, quantised[g][0], quantised[g][1])
